import numpy as np
import ml_dtypes


def mxq(x, axis, fmt="e4m3"):
    dtype, down = {"e4m3": (ml_dtypes.float8_e4m3fn, 7), "e5m2": (ml_dtypes.float8_e5m2, 14)}[fmt]
    v = np.moveaxis(np.asarray(x, np.float32).astype(ml_dtypes.bfloat16).astype(np.float64), axis, -1)
    blocks = v.reshape(v.shape[:-1] + (-1, 32))
    amax = np.abs(blocks).max(-1, keepdims=True)
    byte = np.maximum(np.where(amax > 0, np.frexp(amax)[1] - 1 + 127, 0) - down, 1)
    scale = np.exp2(byte - 127.0)
    codes = (blocks / scale).astype(np.float32).astype(dtype).astype(np.float64)
    return np.moveaxis((codes * scale).reshape(v.shape), -1, axis)


WIDE = False


def mx_kscale(k):
    if not WIDE:
        return np.ones(k)
    levels = np.array([10, -10, 5, -5, 0])
    a = np.random.permutation(np.resize(levels, k // 512 * 4)).reshape(k // 512, 4)
    idx = np.arange(k)
    return np.exp2(a[idx // 512, idx % 128 // 32])


BF16 = ml_dtypes.bfloat16


def bf(x):
    return np.asarray(x, np.float32).astype(BF16)


def f64(x):
    return np.asarray(x).astype(np.float64)


N, H, S, R, T = 4096, 512, 4, 128, 128


def sigmoid(v):
    return 1.0 / (1.0 + np.exp(-v))


def setup_inputs():
    s, t = mx_kscale(H), mx_kscale(H)
    g = np.exp(np.random.standard_normal((S, N)))
    return {"encodings": bf(np.random.standard_normal((N, H)) * s),
            "alphas": bf(g / g.sum(axis=0, keepdims=True)),
            "W1": bf(np.random.standard_normal((S, H, H)) * 1.4 / np.sqrt(H) / s[None, :, None] * t[None, None, :]),
            "b1": bf(np.random.standard_normal((S, H)) * 0.3 * t[None, :]),
            "W2": bf(np.random.standard_normal((S, H, T)) * 2.0 / np.sqrt(H) / t[None, :, None]),
            "b2": bf(np.random.standard_normal((S, T)) * 0.5)}


def reference(encodings, alphas, W1, b1, W2, b2):
    h0 = np.maximum(f64(encodings), 0.0)
    h1 = np.maximum((mxq(h0, 1, "e4m3") @ mxq(f64(W1), 1, "e4m3")) + f64(b1)[:, None, :], 0.0)
    out = sigmoid((mxq(h1, 2, "e4m3") @ mxq(f64(W2), 1, "e4m3")) + f64(b2)[:, None, :])
    return np.sum(f64(alphas)[:, :, None] * out, axis=0)

@@ -1,0 +1,199 @@
+from contextlib import ExitStack
+
+import concourse.bass as bass
+import concourse.mybir as mybir
+import concourse.tile as tile
+from concourse.masks import make_identity
+
+F32 = mybir.dt.float32
+BF16 = mybir.dt.bfloat16
+U32 = mybir.dt.uint32
+U8 = mybir.dt.uint8
+FP8X4 = mybir.dt.float8_e4m3fn_x4
+ACT = mybir.ActivationFunctionType
+ALU = mybir.AluOpType
+
+P = 128
+N_TOK, H, S, T = 4096, 512, 4, 128
+CH = 512
+NB = CH // P
+NCH = N_TOK // CH
+FLOPS = 2 * S * N_TOK * H * (H + T)
+
+
+def tile_moe_pb_kernel(tc, encodings, alphas, W1, b1, W2, b2, out):
+    nc = tc.nc
+    with ExitStack() as ctx:
+        const = ctx.enter_context(tc.tile_pool(name="const", bufs=1))
+        work = ctx.enter_context(tc.tile_pool(name="work", bufs=2))
+        ps1p = ctx.enter_context(tc.psum_pool(name="ps1p", bufs=4))
+        ps2p = ctx.enter_context(tc.psum_pool(name="ps2p", bufs=2))
+        tpp = ctx.enter_context(tc.psum_pool(name="tpp", bufs=2))
+
+        enc_v = encodings.rearrange("(c b p) k -> c p b k", p=P, b=NB)
+        xs = []
+        w1raw = const.tile([P, S, 4, H], BF16)
+        w2raw = const.tile([P, S, 4, T], BF16)
+        small = const.tile([P, P], BF16)
+        alraw = const.tile([P, P], BF16)
+        nc.vector.memset(small[:], 0.0)
+        for c in range(NCH):
+            x_c = const.tile([P, NB, H], BF16, name="x%d" % c)
+            xs.append(x_c)
+
+        def load_w1(s):
+            nc.sync.dma_start(
+                out=w1raw[:, s, :, :].rearrange("p (u e) j -> p u (e j)", u=2),
+                in_=W1[s].rearrange("(u q e) j -> q u (e j)", u=2, e=2),
+            )
+
+        nc.sync.dma_start(out=xs[0][:], in_=enc_v[0])
+        load_w1(0)
+        nc.scalar.dma_start(out=small[0:16, :], in_=b1.rearrange("s (t p) -> (s t) p", p=P))
+        nc.scalar.dma_start(out=small[16:20, :], in_=b2)
+        nc.scalar.dma_start(out=alraw[:], in_=alphas.rearrange("s (n p) -> (s n) p", p=P))
+        nc.sync.dma_start(out=w2raw[:].rearrange("p s t c -> p (s t) c"), in_=W2.rearrange("s (t p) c -> p (s t) c", p=P))
+        load_w1(1)
+        nc.sync.dma_start(out=xs[1][:], in_=enc_v[1])
+        load_w1(2)
+        load_w1(3)
+        for c in range(2, NCH):
+            nc.sync.dma_start(out=xs[c][:], in_=enc_v[c])
+
+        ident_f = const.tile([P, P], F32)
+        make_identity(nc, ident_f[:])
+        ident_b = const.tile([P, P], BF16)
+        make_identity(nc, ident_b[:])
+        scr = const.tile([P, 1], F32)
+        nc.vector.memset(scr[:], 0.0)
+        scr2 = const.tile([P, 1], F32)
+        nc.scalar.activation(out=scr2[:], in_=scr[:], func=ACT.Sigmoid)
+
+        w1w = const.tile([P, S, H], U32, align_bytes=64)
+        w1s = const.tile([P, S, H], U8, align_bytes=64)
+        w2w = const.tile([P, S, T], U32, align_bytes=64)
+        w2s = const.tile([P, S, T], U8, align_bytes=64)
+        h0w = const.tile([P, NCH, CH], U32, align_bytes=64)
+        h0s = const.tile([P, NCH, CH], U8, align_bytes=64)
+        biasT = const.tile([P, 20], F32)
+        alT = const.tile([P, P], F32)
+
+        def prep_h0(c):
+            x_c = xs[c]
+            nc.vector.tensor_scalar_max(out=x_c[:], in0=x_c[:], scalar1=0.0)
+            xw = x_c[:].bitcast(F32)
+            h0g = work.tile([P, CH, 4], BF16, align_bytes=64)
+            h0gw = h0g[:].bitcast(F32)
+            for hb in range(2):
+                tp = tpp.tile([P, 2, 2, P], F32, tag="tp")
+                for b in range(2):
+                    for u in range(2):
+                        nc.tensor.transpose(tp[:, b, u, :], xw[:, 2 * hb + b, P * u : P * u + P], ident_f[:])
+                dst = h0gw[:, 256 * hb : 256 * hb + 256, :].rearrange("p (b n) u -> p b n u", b=2)
+                src = tp[:].rearrange("p b u n -> p b n u")
+                if hb == 0:
+                    nc.vector.tensor_copy(out=dst, in_=src)
+                else:
+                    nc.scalar.copy(out=dst, in_=src)
+            nc.vector.quantize_mx(
+                out=h0w[:, c, :].bitcast(FP8X4),
+                scales=h0s[:, c, :],
+                in_=h0g[:].rearrange("p n t -> p (n t)"),
+            )
+
+        def prep_w1(s):
+            w1g = work.tile([P, H, 4], BF16, align_bytes=64)
+            nc.vector.tensor_copy(
+                out=w1g[:].rearrange("p (c i) t -> p c t i", i=4),
+                in_=w1raw[:, s, :, :].rearrange("p t (c i) -> p c t i", i=4),
+            )
+            nc.vector.quantize_mx(
+                out=w1w[:, s, :].bitcast(FP8X4),
+                scales=w1s[:, s, :],
+                in_=w1g[:].rearrange("p n t -> p (n t)"),
+            )
+
+        def prep_w2():
+            w2g = const.tile([P, S, T, 4], BF16, align_bytes=64)
+            nc.vector.tensor_copy(out=w2g[:], in_=w2raw[:].rearrange("p s t c -> p s c t"))
+            nc.vector.quantize_mx(
+                out=w2w[:].rearrange("p s c -> p (s c)").bitcast(FP8X4),
+                scales=w2s[:].rearrange("p s c -> p (s c)"),
+                in_=w2g[:].rearrange("p s c t -> p (s c t)"),
+            )
+
+        def prep_small():
+            tb = tpp.tile([P, P], BF16, tag="tp")
+            nc.tensor.transpose(tb[:], small[:], ident_b[:])
+            nc.vector.tensor_copy(out=biasT[:], in_=tb[:, 0:20])
+            ta = tpp.tile([P, P], BF16, tag="tp")
+            nc.tensor.transpose(ta[:], alraw[:], ident_b[:])
+            nc.vector.tensor_copy(out=alT[:], in_=ta[:])
+
+        out_v = out.rearrange("(c b p) t -> c p b t", p=P, b=NB)
+
+        prep_h0(0)
+        prep_w1(0)
+        prep_small()
+        prep_w2()
+
+        for c in range(NCH):
+            acc = work.tile([P, NB, T], F32)
+            for s in range(S):
+                if c == 0 and s + 1 < S:
+                    prep_w1(s + 1)
+                if s == 1 and c + 1 < NCH:
+                    prep_h0(c + 1)
+                planar = work.tile([P, 4, CH], BF16)
+                for t in range(4):
+                    ps1 = ps1p.tile([P, CH], F32)
+                    nc.tensor.matmul_mx(
+                        out=ps1[:],
+                        lhsT=w1w[:, s, P * t : P * t + P].bitcast(FP8X4),
+                        lhsT_scale=w1s[:, s, P * t : P * t + P],
+                        rhs=h0w[:, c, :].bitcast(FP8X4),
+                        rhs_scale=h0s[:, c, :],
+                        start=True,
+                        stop=True,
+                    )
+                    nc.scalar.activation(
+                        out=planar[:, t, :], in_=ps1[:], func=ACT.Relu,
+                        bias=biasT[:, 4 * s + t : 4 * s + t + 1], scale=1.0,
+                    )
+                h1g = work.tile([P, CH, 4], BF16, align_bytes=64)
+                nc.vector.tensor_copy(
+                    out=h1g[:].rearrange("p (c i) t -> p c t i", i=4),
+                    in_=planar[:].rearrange("p t (c i) -> p c t i", i=4),
+                )
+                h1w = work.tile([P, CH], U32, align_bytes=64)
+                h1s = work.tile([P, CH], U8, align_bytes=64)
+                nc.vector.quantize_mx(
+                    out=h1w[:].bitcast(FP8X4), scales=h1s[:], in_=h1g[:].rearrange("p n t -> p (n t)")
+                )
+                ps2 = ps2p.tile([P, CH], F32)
+                nc.tensor.matmul_mx(
+                    out=ps2[:],
+                    lhsT=w2w[:, s, :].bitcast(FP8X4),
+                    lhsT_scale=w2s[:, s, :],
+                    rhs=h1w[:].bitcast(FP8X4),
+                    rhs_scale=h1s[:],
+                    start=True,
+                    stop=True,
+                )
+                prob = work.tile([P, CH], F32)
+                nc.scalar.activation(
+                    out=prob[:], in_=ps2[:], func=ACT.Sigmoid, bias=biasT[:, 16 + s : 17 + s], scale=1.0
+                )
+                tq = tpp.tile([P, NB, T], F32, tag="tp")
+                for b in range(NB):
+                    nc.tensor.transpose(tq[:, b, :], prob[:, P * b : P * b + P], ident_f[:])
+                for b in range(NB):
+                    col = 32 * s + NB * c + b
+                    if s == 0:
+                        nc.vector.tensor_scalar_mul(out=acc[:, b, :], in0=tq[:, b, :], scalar1=alT[:, col : col + 1])
+                    else:
+                        nc.vector.scalar_tensor_tensor(
+                            out=acc[:, b, :], in0=tq[:, b, :], scalar=alT[:, col : col + 1], in1=acc[:, b, :],
+                            op0=ALU.mult, op1=ALU.add,
+                        )
+            nc.sync.dma_start(out=out_v[c], in_=acc[:])

@@ -1,8 +1,6 @@
 from contextlib import ExitStack
 
-import concourse.bass as bass
 import concourse.mybir as mybir
-import concourse.tile as tile
 from concourse.masks import make_identity
 
 F32 = mybir.dt.float32
@@ -18,25 +16,32 @@ N_TOK, H, S, T = 4096, 512, 4, 128
 CH = 512
 NB = CH // P
 NCH = N_TOK // CH
+NU = NCH * S
 FLOPS = 2 * S * N_TOK * H * (H + T)
 
 
 def tile_moe_pb_kernel(tc, encodings, alphas, W1, b1, W2, b2, out):
     nc = tc.nc
     with ExitStack() as ctx:
+        ctx.enter_context(tc.manual_schedule())
         const = ctx.enter_context(tc.tile_pool(name="const", bufs=1))
         work = ctx.enter_context(tc.tile_pool(name="work", bufs=2))
         ps1p = ctx.enter_context(tc.psum_pool(name="ps1p", bufs=4))
-        ps2p = ctx.enter_context(tc.psum_pool(name="ps2p", bufs=2))
+        ps2p = ctx.enter_context(tc.psum_pool(name="ps2p", bufs=1))
+        tqp = ctx.enter_context(tc.psum_pool(name="tqp", bufs=1))
         tpp = ctx.enter_context(tc.psum_pool(name="tpp", bufs=2))
 
         enc_v = encodings.rearrange("(c b p) k -> c p b k", p=P, b=NB)
+        out_v = out.rearrange("(c b p) t -> c p b t", p=P, b=NB)
         xs = []
         w1raw = const.tile([P, S, 4, H], BF16)
         w2raw = const.tile([P, S, 4, T], BF16)
         small = const.tile([P, P], BF16)
         alraw = const.tile([P, P], BF16)
+        scr = const.tile([P, 1], F32)
+        scr2 = const.tile([P, 1], F32)
         nc.vector.memset(small[:], 0.0)
+        nc.vector.memset(scr[:], 0.0)
         for c in range(NCH):
             x_c = const.tile([P, NB, H], BF16, name="x%d" % c)
             xs.append(x_c)
@@ -47,15 +52,16 @@ def tile_moe_pb_kernel(tc, encodings, alphas, W1, b1, W2, b2, out):
                 in_=W1[s].rearrange("(u q e) j -> q u (e j)", u=2, e=2),
             )
 
-        nc.sync.dma_start(out=xs[0][:], in_=enc_v[0])
-        load_w1(0)
         nc.scalar.dma_start(out=small[0:16, :], in_=b1.rearrange("s (t p) -> (s t) p", p=P))
         nc.scalar.dma_start(out=small[16:20, :], in_=b2)
         nc.scalar.dma_start(out=alraw[:], in_=alphas.rearrange("s (n p) -> (s n) p", p=P))
-        nc.sync.dma_start(out=w2raw[:].rearrange("p s t c -> p (s t) c"), in_=W2.rearrange("s (t p) c -> p (s t) c", p=P))
+        nc.sync.dma_start(out=xs[0][:, 0:2, :], in_=enc_v[0][:, 0:2, :])
+        nc.sync.dma_start(out=xs[0][:, 2:4, :], in_=enc_v[0][:, 2:4, :])
+        load_w1(0)
         load_w1(1)
-        nc.sync.dma_start(out=xs[1][:], in_=enc_v[1])
+        nc.sync.dma_start(out=w2raw[:].rearrange("p s t c -> p (s t) c"), in_=W2.rearrange("s (t p) c -> p (s t) c", p=P))
         load_w1(2)
+        nc.sync.dma_start(out=xs[1][:], in_=enc_v[1])
         load_w1(3)
         for c in range(2, NCH):
             nc.sync.dma_start(out=xs[c][:], in_=enc_v[c])
@@ -64,136 +70,219 @@ def tile_moe_pb_kernel(tc, encodings, alphas, W1, b1, W2, b2, out):
         make_identity(nc, ident_f[:])
         ident_b = const.tile([P, P], BF16)
         make_identity(nc, ident_b[:])
-        scr = const.tile([P, 1], F32)
-        nc.vector.memset(scr[:], 0.0)
-        scr2 = const.tile([P, 1], F32)
         nc.scalar.activation(out=scr2[:], in_=scr[:], func=ACT.Sigmoid)
 
         w1w = const.tile([P, S, H], U32, align_bytes=64)
         w1s = const.tile([P, S, H], U8, align_bytes=64)
         w2w = const.tile([P, S, T], U32, align_bytes=64)
         w2s = const.tile([P, S, T], U8, align_bytes=64)
+        w2g = const.tile([P, S, T, 4], BF16, align_bytes=64)
         h0w = const.tile([P, NCH, CH], U32, align_bytes=64)
         h0s = const.tile([P, NCH, CH], U8, align_bytes=64)
         biasT = const.tile([P, 20], F32)
         alT = const.tile([P, P], F32)
 
-        def prep_h0(c):
-            x_c = xs[c]
-            nc.vector.tensor_scalar_max(out=x_c[:], in0=x_c[:], scalar1=0.0)
-            xw = x_c[:].bitcast(F32)
-            h0g = work.tile([P, CH, 4], BF16, align_bytes=64)
-            h0gw = h0g[:].bitcast(F32)
+        st = {}
+
+        def h0_relu(c, lo=0, hi=NB):
+            nc.vector.tensor_scalar_max(out=xs[c][:, lo:hi, :], in0=xs[c][:, lo:hi, :], scalar1=0.0)
+
+        def h0_transposes(c):
+            xw = xs[c][:].bitcast(F32)
             for hb in range(2):
-                tp = tpp.tile([P, 2, 2, P], F32, tag="tp")
+                tp = tpp.tile([P, 2, 2, P], F32, tag="tp", name="tp")
+                st[("tp", c, hb)] = tp
                 for b in range(2):
                     for u in range(2):
                         nc.tensor.transpose(tp[:, b, u, :], xw[:, 2 * hb + b, P * u : P * u + P], ident_f[:])
-                dst = h0gw[:, 256 * hb : 256 * hb + 256, :].rearrange("p (b n) u -> p b n u", b=2)
-                src = tp[:].rearrange("p b u n -> p b n u")
-                if hb == 0:
-                    nc.vector.tensor_copy(out=dst, in_=src)
-                else:
-                    nc.scalar.copy(out=dst, in_=src)
+            st[("h0g", c)] = work.tile([P, CH, 4], BF16, align_bytes=64, tag="h0g", name="h0g")
+
+        def h0_evac(c, hb, eng):
+            h0gw = st[("h0g", c)][:].bitcast(F32)
+            dst = h0gw[:, 256 * hb : 256 * hb + 256, :].rearrange("p (b n) u -> p b n u", b=2)
+            src = st[("tp", c, hb)][:].rearrange("p b u n -> p b n u")
+            if eng == "S":
+                nc.scalar.copy(out=dst, in_=src)
+            else:
+                nc.vector.tensor_copy(out=dst, in_=src)
+
+        def h0_quant(c, lo=0, hi=CH):
             nc.vector.quantize_mx(
-                out=h0w[:, c, :].bitcast(FP8X4),
-                scales=h0s[:, c, :],
-                in_=h0g[:].rearrange("p n t -> p (n t)"),
+                out=h0w[:, c, lo:hi].bitcast(FP8X4),
+                scales=h0s[:, c, lo:hi],
+                in_=st[("h0g", c)][:, lo:hi, :].rearrange("p n t -> p (n t)"),
             )
 
-        def prep_w1(s):
-            w1g = work.tile([P, H, 4], BF16, align_bytes=64)
+        def w1_regroup(s, lo=0, hi=H):
+            if lo == 0:
+                st[("w1g", s)] = work.tile([P, H, 4], BF16, align_bytes=64, tag="w1g", name="w1g")
             nc.vector.tensor_copy(
-                out=w1g[:].rearrange("p (c i) t -> p c t i", i=4),
-                in_=w1raw[:, s, :, :].rearrange("p t (c i) -> p c t i", i=4),
-            )
-            nc.vector.quantize_mx(
-                out=w1w[:, s, :].bitcast(FP8X4),
-                scales=w1s[:, s, :],
-                in_=w1g[:].rearrange("p n t -> p (n t)"),
+                out=st[("w1g", s)][:, lo:hi, :].rearrange("p (c i) t -> p c t i", i=4),
+                in_=w1raw[:, s, :, lo:hi].rearrange("p t (c i) -> p c t i", i=4),
             )
 
-        def prep_w2():
-            w2g = const.tile([P, S, T, 4], BF16, align_bytes=64)
+        def w1_quant(s, lo=0, hi=H):
+            nc.vector.quantize_mx(
+                out=w1w[:, s, lo:hi].bitcast(FP8X4),
+                scales=w1s[:, s, lo:hi],
+                in_=st[("w1g", s)][:, lo:hi, :].rearrange("p n t -> p (n t)"),
+            )
+
+        def w2_regroup():
             nc.vector.tensor_copy(out=w2g[:], in_=w2raw[:].rearrange("p s t c -> p s c t"))
+
+        def w2_quant():
             nc.vector.quantize_mx(
                 out=w2w[:].rearrange("p s c -> p (s c)").bitcast(FP8X4),
                 scales=w2s[:].rearrange("p s c -> p (s c)"),
                 in_=w2g[:].rearrange("p s c t -> p (s c t)"),
             )
 
-        def prep_small():
-            tb = tpp.tile([P, P], BF16, tag="tp")
-            nc.tensor.transpose(tb[:], small[:], ident_b[:])
-            nc.vector.tensor_copy(out=biasT[:], in_=tb[:, 0:20])
-            ta = tpp.tile([P, P], BF16, tag="tp")
-            nc.tensor.transpose(ta[:], alraw[:], ident_b[:])
-            nc.vector.tensor_copy(out=alT[:], in_=ta[:])
+        def mx1(k, t):
+            c, s = divmod(k, S)
+            ps1 = ps1p.tile([P, CH], F32, tag="ps1", name="ps1")
+            st[("ps1", k, t)] = ps1
+            nc.tensor.matmul_mx(
+                out=ps1[:],
+                lhsT=w1w[:, s, P * t : P * t + P].bitcast(FP8X4),
+                lhsT_scale=w1s[:, s, P * t : P * t + P],
+                rhs=h0w[:, c, :].bitcast(FP8X4),
+                rhs_scale=h0s[:, c, :],
+                start=True,
+                stop=True,
+            )
 
-        out_v = out.rearrange("(c b p) t -> c p b t", p=P, b=NB)
+        def ev(k, t):
+            s = k % S
+            if t == 0:
+                st[("planar", k)] = work.tile([P, 4, CH], BF16, tag="planar", name="planar", bufs=4)
+            nc.scalar.activation(
+                out=st[("planar", k)][:, t, :], in_=st[("ps1", k, t)][:], func=ACT.Relu,
+                bias=biasT[:, 4 * s + t : 4 * s + t + 1], scale=1.0,
+            )
 
-        prep_h0(0)
-        prep_w1(0)
-        prep_small()
-        prep_w2()
+        def rg(k):
+            h1g = work.tile([P, CH, 4], BF16, align_bytes=64, tag="h1g", name="h1g", bufs=2)
+            st[("h1g", k)] = h1g
+            nc.vector.tensor_copy(
+                out=h1g[:].rearrange("p (c i) t -> p c t i", i=4),
+                in_=st[("planar", k)][:].rearrange("p t (c i) -> p c t i", i=4),
+            )
 
-        for c in range(NCH):
-            acc = work.tile([P, NB, T], F32)
-            for s in range(S):
-                if c == 0 and s + 1 < S:
-                    prep_w1(s + 1)
-                if s == 1 and c + 1 < NCH:
-                    prep_h0(c + 1)
-                planar = work.tile([P, 4, CH], BF16)
-                for t in range(4):
-                    ps1 = ps1p.tile([P, CH], F32)
-                    nc.tensor.matmul_mx(
-                        out=ps1[:],
-                        lhsT=w1w[:, s, P * t : P * t + P].bitcast(FP8X4),
-                        lhsT_scale=w1s[:, s, P * t : P * t + P],
-                        rhs=h0w[:, c, :].bitcast(FP8X4),
-                        rhs_scale=h0s[:, c, :],
-                        start=True,
-                        stop=True,
+        def qu(k):
+            h1w = work.tile([P, CH], U32, align_bytes=64, tag="h1w", name="h1w", bufs=3)
+            h1s = work.tile([P, CH], U8, align_bytes=64, tag="h1s", name="h1s", bufs=3)
+            st[("h1w", k)] = h1w
+            st[("h1s", k)] = h1s
+            nc.vector.quantize_mx(
+                out=h1w[:].bitcast(FP8X4), scales=h1s[:], in_=st[("h1g", k)][:].rearrange("p n t -> p (n t)")
+            )
+
+        def mx2(k):
+            s = k % S
+            ps2 = ps2p.tile([P, CH], F32, tag="ps2", name="ps2")
+            st[("ps2", k)] = ps2
+            nc.tensor.matmul_mx(
+                out=ps2[:],
+                lhsT=w2w[:, s, :].bitcast(FP8X4),
+                lhsT_scale=w2s[:, s, :],
+                rhs=st[("h1w", k)][:].bitcast(FP8X4),
+                rhs_scale=st[("h1s", k)][:],
+                start=True,
+                stop=True,
+            )
+
+        def sg(k):
+            s = k % S
+            prob = work.tile([P, CH], F32, tag="prob", name="prob", bufs=2)
+            st[("prob", k)] = prob
+            nc.scalar.activation(
+                out=prob[:], in_=st[("ps2", k)][:], func=ACT.Sigmoid, bias=biasT[:, 16 + s : 17 + s], scale=1.0
+            )
+
+        def tr(k):
+            tq = tqp.tile([P, NB, T], F32, tag="tq", name="tq")
+            st[("tq", k)] = tq
+            for b in range(NB):
+                nc.tensor.transpose(tq[:, b, :], st[("prob", k)][:, P * b : P * b + P], ident_f[:])
+
+        def mix(k):
+            c, s = divmod(k, S)
+            if s == 0:
+                st[("acc", c)] = work.tile([P, NB, T], F32, tag="acc", name="acc")
+            acc = st[("acc", c)]
+            tq = st[("tq", k)]
+            for b in range(NB):
+                col = 32 * s + NB * c + b
+                if s == 0:
+                    nc.vector.tensor_scalar_mul(out=acc[:, b, :], in0=tq[:, b, :], scalar1=alT[:, col : col + 1])
+                else:
+                    nc.vector.scalar_tensor_tensor(
+                        out=acc[:, b, :], in0=tq[:, b, :], scalar=alT[:, col : col + 1], in1=acc[:, b, :],
+                        op0=ALU.mult, op1=ALU.add,
                     )
-                    nc.scalar.activation(
-                        out=planar[:, t, :], in_=ps1[:], func=ACT.Relu,
-                        bias=biasT[:, 4 * s + t : 4 * s + t + 1], scale=1.0,
-                    )
-                h1g = work.tile([P, CH, 4], BF16, align_bytes=64)
-                nc.vector.tensor_copy(
-                    out=h1g[:].rearrange("p (c i) t -> p c t i", i=4),
-                    in_=planar[:].rearrange("p t (c i) -> p c t i", i=4),
-                )
-                h1w = work.tile([P, CH], U32, align_bytes=64)
-                h1s = work.tile([P, CH], U8, align_bytes=64)
-                nc.vector.quantize_mx(
-                    out=h1w[:].bitcast(FP8X4), scales=h1s[:], in_=h1g[:].rearrange("p n t -> p (n t)")
-                )
-                ps2 = ps2p.tile([P, CH], F32)
-                nc.tensor.matmul_mx(
-                    out=ps2[:],
-                    lhsT=w2w[:, s, :].bitcast(FP8X4),
-                    lhsT_scale=w2s[:, s, :],
-                    rhs=h1w[:].bitcast(FP8X4),
-                    rhs_scale=h1s[:],
-                    start=True,
-                    stop=True,
-                )
-                prob = work.tile([P, CH], F32)
-                nc.scalar.activation(
-                    out=prob[:], in_=ps2[:], func=ACT.Sigmoid, bias=biasT[:, 16 + s : 17 + s], scale=1.0
-                )
-                tq = tpp.tile([P, NB, T], F32, tag="tp")
-                for b in range(NB):
-                    nc.tensor.transpose(tq[:, b, :], prob[:, P * b : P * b + P], ident_f[:])
-                for b in range(NB):
-                    col = 32 * s + NB * c + b
-                    if s == 0:
-                        nc.vector.tensor_scalar_mul(out=acc[:, b, :], in0=tq[:, b, :], scalar1=alT[:, col : col + 1])
-                    else:
-                        nc.vector.scalar_tensor_tensor(
-                            out=acc[:, b, :], in0=tq[:, b, :], scalar=alT[:, col : col + 1], in1=acc[:, b, :],
-                            op0=ALU.mult, op1=ALU.add,
-                        )
-            nc.sync.dma_start(out=out_v[c], in_=acc[:])
+            if s == S - 1:
+                nc.sync.dma_start(out=out_v[c], in_=acc[:])
+
+        h0_relu(0, 0, 2)
+        h0_relu(0, 2, 4)
+        h0_transposes(0)
+        tb = ps2p.tile([P, P], BF16, tag="ps2", name="tb")
+        nc.tensor.transpose(tb[:], small[:], ident_b[:])
+        ta = tqp.tile([P, P], BF16, tag="tq", name="ta")
+        nc.tensor.transpose(ta[:], alraw[:], ident_b[:])
+        h0_evac(0, 0, "S")
+        h0_evac(0, 1, "S")
+        nc.vector.tensor_copy(out=biasT[:], in_=tb[:, 0:20])
+        w1_regroup(0, 0, 128)
+        h0_quant(0, 0, 256)
+        w1_regroup(0, 128, 256)
+        h0_quant(0, 256, 512)
+        w1_quant(0, 0, 128)
+        w1_regroup(0, 256, 384)
+        w1_quant(0, 128, 256)
+        w1_regroup(0, 384, 512)
+        w1_quant(0, 256, 384)
+        nc.vector.tensor_copy(out=alT[:], in_=ta[:])
+        w1_quant(0, 384, 512)
+        for t in range(4):
+            mx1(0, t)
+
+        for k in range(NU + 3):
+            c, s = divmod(k, S)
+            nxt = c + 1 if (k < NU and c + 1 < NCH) else None
+            if 0 <= k - 3 < NU:
+                tr(k - 3)
+            if nxt is not None and s == 2:
+                h0_transposes(nxt)
+            if 0 <= k - 2 < NU:
+                mx2(k - 2)
+            if k + 1 < S:
+                w1_regroup(k + 1)
+            if 0 <= k - 1 < NU:
+                rg(k - 1)
+            if k == 1:
+                w2_regroup()
+            if nxt is not None and s == 3:
+                h0_quant(nxt)
+            if k + 1 < S:
+                w1_quant(k + 1)
+            for t in range(4):
+                if k < NU:
+                    ev(k, t)
+                if k + 1 < NU:
+                    mx1(k + 1, t)
+            if 0 <= k - 3 < NU:
+                mix(k - 3)
+            if nxt is not None and s == 2:
+                engs = ("V", "S")
+                h0_evac(nxt, 0, engs[0])
+                h0_evac(nxt, 1, engs[1])
+            if 0 <= k - 1 < NU:
+                qu(k - 1)
+            if k == 1:
+                w2_quant()
+            if nxt is not None and s == 1:
+                h0_relu(nxt)
+            if 0 <= k - 2 < NU:
+                sg(k - 2)

@@ -84,9 +84,6 @@ def tile_moe_pb_kernel(tc, encodings, alphas, W1, b1, W2, b2, out):
 
         st = {}
 
-        def h0_relu(c, lo=0, hi=NB):
-            nc.vector.tensor_scalar_max(out=xs[c][:, lo:hi, :], in0=xs[c][:, lo:hi, :], scalar1=0.0)
-
         def h0_transposes(c):
             xw = xs[c][:].bitcast(F32)
             for hb in range(2):
@@ -98,13 +95,16 @@ def tile_moe_pb_kernel(tc, encodings, alphas, W1, b1, W2, b2, out):
             st[("h0g", c)] = work.tile([P, CH, 4], BF16, align_bytes=64, tag="h0g", name="h0g")
 
         def h0_evac(c, hb, eng):
-            h0gw = st[("h0g", c)][:].bitcast(F32)
-            dst = h0gw[:, 256 * hb : 256 * hb + 256, :].rearrange("p (b n) u -> p b n u", b=2)
-            src = st[("tp", c, hb)][:].rearrange("p b u n -> p b n u")
-            if eng == "S":
-                nc.scalar.copy(out=dst, in_=src)
-            else:
-                nc.vector.tensor_copy(out=dst, in_=src)
+            h0g = st[("h0g", c)]
+            tpb = st[("tp", c, hb)][:].bitcast(BF16)
+            for b in range(2):
+                n0 = P * (2 * hb + b)
+                dst = h0g[:, n0 : n0 + P, :].rearrange("p n (u e) -> p n u e", u=2)
+                src = tpb[:, b, :, :].rearrange("p u (n e) -> p n u e", e=2)
+                if eng == "S":
+                    nc.scalar.activation(out=dst, in_=src, func=ACT.Relu)
+                else:
+                    nc.vector.tensor_scalar_max(out=dst, in0=src, scalar1=0.0)
 
         def h0_quant(c, lo=0, hi=CH):
             nc.vector.quantize_mx(
@@ -224,14 +224,12 @@ def tile_moe_pb_kernel(tc, encodings, alphas, W1, b1, W2, b2, out):
             if s == S - 1:
                 nc.sync.dma_start(out=out_v[c], in_=acc[:])
 
-        h0_relu(0, 0, 2)
-        h0_relu(0, 2, 4)
         h0_transposes(0)
         tb = ps2p.tile([P, P], BF16, tag="ps2", name="tb")
         nc.tensor.transpose(tb[:], small[:], ident_b[:])
         ta = tqp.tile([P, P], BF16, tag="tq", name="ta")
         nc.tensor.transpose(ta[:], alraw[:], ident_b[:])
-        h0_evac(0, 0, "S")
+        h0_evac(0, 0, "V")
         h0_evac(0, 1, "S")
         nc.vector.tensor_copy(out=biasT[:], in_=tb[:, 0:20])
         w1_regroup(0, 0, 128)
@@ -275,14 +273,12 @@ def tile_moe_pb_kernel(tc, encodings, alphas, W1, b1, W2, b2, out):
             if 0 <= k - 3 < NU:
                 mix(k - 3)
             if nxt is not None and s == 2:
-                engs = ("V", "S")
+                engs = ("V", "V")
                 h0_evac(nxt, 0, engs[0])
                 h0_evac(nxt, 1, engs[1])
             if 0 <= k - 1 < NU:
                 qu(k - 1)
             if k == 1:
                 w2_quant()
-            if nxt is not None and s == 1:
-                h0_relu(nxt)
             if 0 <= k - 2 < NU:
                 sg(k - 2)

@@ -129,7 +129,7 @@ def tile_moe_pb_kernel(tc, encodings, alphas, W1, b1, W2, b2, out):
             )
 
         def w2_regroup():
-            nc.vector.tensor_copy(out=w2g[:], in_=w2raw[:].rearrange("p s t c -> p s c t"))
+            nc.scalar.copy(out=w2g[:], in_=w2raw[:].rearrange("p s t c -> p s c t"))
 
         def w2_quant():
             nc.vector.quantize_mx(
@@ -232,11 +232,11 @@ def tile_moe_pb_kernel(tc, encodings, alphas, W1, b1, W2, b2, out):
         h0_evac(0, 0, "V")
         h0_evac(0, 1, "S")
         nc.vector.tensor_copy(out=biasT[:], in_=tb[:, 0:20])
-        w1_regroup(0, 0, 128)
         h0_quant(0, 0, 256)
-        w1_regroup(0, 128, 256)
+        w1_regroup(0, 0, 128)
         h0_quant(0, 256, 512)
         w1_quant(0, 0, 128)
+        w1_regroup(0, 128, 256)
         w1_regroup(0, 256, 384)
         w1_quant(0, 128, 256)
         w1_regroup(0, 384, 512)
@@ -251,7 +251,7 @@ def tile_moe_pb_kernel(tc, encodings, alphas, W1, b1, W2, b2, out):
             nxt = c + 1 if (k < NU and c + 1 < NCH) else None
             if 0 <= k - 3 < NU:
                 tr(k - 3)
-            if nxt is not None and s == 2:
+            if nxt is not None and s == (2 if c == 0 else 1):
                 h0_transposes(nxt)
             if 0 <= k - 2 < NU:
                 mx2(k - 2)
@@ -261,7 +261,7 @@ def tile_moe_pb_kernel(tc, encodings, alphas, W1, b1, W2, b2, out):
                 rg(k - 1)
             if k == 1:
                 w2_regroup()
-            if nxt is not None and s == 3:
+            if nxt is not None and s == (3 if c == 0 else 2):
                 h0_quant(nxt)
             if k + 1 < S:
                 w1_quant(k + 1)
@@ -272,7 +272,7 @@ def tile_moe_pb_kernel(tc, encodings, alphas, W1, b1, W2, b2, out):
                     mx1(k + 1, t)
             if 0 <= k - 3 < NU:
                 mix(k - 3)
-            if nxt is not None and s == 2:
+            if nxt is not None and s == (2 if c == 0 else 1):
                 engs = ("V", "V")
                 h0_evac(nxt, 0, engs[0])
                 h0_evac(nxt, 1, engs[1])

@@ -214,7 +214,9 @@ def tile_moe_pb_kernel(tc, encodings, alphas, W1, b1, W2, b2, out):
             tq = st[("tq", k)]
             for b in range(NB):
                 col = 32 * s + NB * c + b
-                if s == 0:
+                if s == 0 and c % 2 == 0:
+                    nc.scalar.activation(out=acc[:, b, :], in_=tq[:, b, :], func=ACT.Copy, scale=alT[:, col : col + 1])
+                elif s == 0:
                     nc.vector.tensor_scalar_mul(out=acc[:, b, :], in0=tq[:, b, :], scalar1=alT[:, col : col + 1])
                 else:
                     nc.vector.scalar_tensor_tensor(

@@ -12,11 +12,12 @@ ACT = mybir.ActivationFunctionType
 ALU = mybir.AluOpType
 
 P = 128
+PACK = 4
 N_TOK, H, S, T = 4096, 512, 4, 128
-CH = 512
-NB = CH // P
-NCH = N_TOK // CH
-NU = NCH * S
+CHUNK = 512
+BLOCKS = CHUNK // P
+N_CHUNKS = N_TOK // CHUNK
+HALF = CHUNK // 2
 FLOPS = 2 * S * N_TOK * H * (H + T)
 
 
@@ -26,24 +27,34 @@ def tile_moe_pb_kernel(tc, encodings, alphas, W1, b1, W2, b2, out):
         ctx.enter_context(tc.manual_schedule())
         const = ctx.enter_context(tc.tile_pool(name="const", bufs=1))
         work = ctx.enter_context(tc.tile_pool(name="work", bufs=2))
-        ps1p = ctx.enter_context(tc.psum_pool(name="ps1p", bufs=4))
-        ps2p = ctx.enter_context(tc.psum_pool(name="ps2p", bufs=1))
-        tqp = ctx.enter_context(tc.psum_pool(name="tqp", bufs=1))
-        tpp = ctx.enter_context(tc.psum_pool(name="tpp", bufs=2))
+        bank1 = ctx.enter_context(tc.psum_pool(name="bank1", bufs=PACK))
+        bank2 = ctx.enter_context(tc.psum_pool(name="bank2", bufs=1))
+        bankp = ctx.enter_context(tc.psum_pool(name="bankp", bufs=1))
+        bankx = ctx.enter_context(tc.psum_pool(name="bankx", bufs=2))
 
-        enc_v = encodings.rearrange("(c b p) k -> c p b k", p=P, b=NB)
-        out_v = out.rearrange("(c b p) t -> c p b t", p=P, b=NB)
-        xs = []
-        w1raw = const.tile([P, S, 4, H], BF16)
-        w2raw = const.tile([P, S, 4, T], BF16)
+        units = []
+        for c in range(N_CHUNKS):
+            for s in range(S):
+                if c == N_CHUNKS - 1 and s == S - 1:
+                    units.append((c, s, 0, HALF))
+                    units.append((c, s, HALF, HALF))
+                else:
+                    units.append((c, s, 0, CHUNK))
+        n_whole = len(units) - 2
+
+        enc_v = encodings.rearrange("(c b p) k -> c p b k", p=P, b=BLOCKS)
+        out_v = out.rearrange("(c b p) t -> c p b t", p=P, b=BLOCKS)
+        w1raw = const.tile([P, S, PACK, H], BF16)
+        w2raw = const.tile([P, S, PACK, T], BF16)
         small = const.tile([P, P], BF16)
         alraw = const.tile([P, P], BF16)
-        scr = const.tile([P, 1], F32)
-        scr2 = const.tile([P, 1], F32)
+        zero = const.tile([P, 1], F32)
+        warm = const.tile([P, 1], F32)
         nc.vector.memset(small[:], 0.0)
-        nc.vector.memset(scr[:], 0.0)
-        for c in range(NCH):
-            x_c = const.tile([P, NB, H], BF16, name="x%d" % c)
+        nc.vector.memset(zero[:], 0.0)
+        xs = []
+        for c in range(N_CHUNKS):
+            x_c = const.tile([P, BLOCKS, H], BF16, name="x%d" % c)
             xs.append(x_c)
 
         def load_w1(s):
@@ -59,73 +70,78 @@ def tile_moe_pb_kernel(tc, encodings, alphas, W1, b1, W2, b2, out):
         nc.sync.dma_start(out=xs[0][:, 2:4, :], in_=enc_v[0][:, 2:4, :])
         load_w1(0)
         load_w1(1)
-        nc.sync.dma_start(out=w2raw[:].rearrange("p s t c -> p (s t) c"), in_=W2.rearrange("s (t p) c -> p (s t) c", p=P))
+        nc.sync.dma_start(
+            out=w2raw[:].rearrange("p s t c -> p (s t) c"), in_=W2.rearrange("s (t p) c -> p (s t) c", p=P)
+        )
         load_w1(2)
         nc.sync.dma_start(out=xs[1][:], in_=enc_v[1])
         load_w1(3)
-        for c in range(2, NCH):
+        for c in range(2, N_CHUNKS):
             nc.sync.dma_start(out=xs[c][:], in_=enc_v[c])
 
         ident_f = const.tile([P, P], F32)
         make_identity(nc, ident_f[:])
         ident_b = const.tile([P, P], BF16)
         make_identity(nc, ident_b[:])
-        nc.scalar.activation(out=scr2[:], in_=scr[:], func=ACT.Sigmoid)
+        nc.scalar.activation(out=warm[:], in_=zero[:], func=ACT.Sigmoid)
 
         w1w = const.tile([P, S, H], U32, align_bytes=64)
         w1s = const.tile([P, S, H], U8, align_bytes=64)
         w2w = const.tile([P, S, T], U32, align_bytes=64)
         w2s = const.tile([P, S, T], U8, align_bytes=64)
-        w2g = const.tile([P, S, T, 4], BF16, align_bytes=64)
-        h0w = const.tile([P, NCH, CH], U32, align_bytes=64)
-        h0s = const.tile([P, NCH, CH], U8, align_bytes=64)
+        w2g = const.tile([P, S, T, PACK], BF16, align_bytes=64)
+        h0w = const.tile([P, N_CHUNKS, CHUNK], U32, align_bytes=64)
+        h0s = const.tile([P, N_CHUNKS, CHUNK], U8, align_bytes=64)
         biasT = const.tile([P, 20], F32)
         alT = const.tile([P, P], F32)
 
-        st = {}
+        live = {}
 
         def h0_transposes(c):
-            xw = xs[c][:].bitcast(F32)
-            for hb in range(2):
-                tp = tpp.tile([P, 2, 2, P], F32, tag="tp", name="tp")
-                st[("tp", c, hb)] = tp
+            words = xs[c][:].bitcast(F32)
+            for pair in range(2):
+                turned = bankx.tile([P, 2, 2, P], F32, tag="turned", name="turned")
+                live[("turned", c, pair)] = turned
                 for b in range(2):
                     for u in range(2):
-                        nc.tensor.transpose(tp[:, b, u, :], xw[:, 2 * hb + b, P * u : P * u + P], ident_f[:])
-            st[("h0g", c)] = work.tile([P, CH, 4], BF16, align_bytes=64, tag="h0g", name="h0g")
+                        nc.tensor.transpose(
+                            turned[:, b, u, :], words[:, 2 * pair + b, P * u : P * u + P], ident_f[:]
+                        )
+            live[("h0g", c)] = work.tile([P, CHUNK, PACK], BF16, align_bytes=64, tag="h0g", name="h0g")
 
-        def h0_evac(c, hb, eng):
-            h0g = st[("h0g", c)]
-            tpb = st[("tp", c, hb)][:].bitcast(BF16)
+        def h0_copy(c, pair, on_scalar):
+            view = live[("turned", c, pair)][:].bitcast(BF16)
             for b in range(2):
-                n0 = P * (2 * hb + b)
-                dst = h0g[:, n0 : n0 + P, :].rearrange("p n (u e) -> p n u e", u=2)
-                src = tpb[:, b, :, :].rearrange("p u (n e) -> p n u e", e=2)
-                if eng == "S":
+                n0 = P * (2 * pair + b)
+                dst = live[("h0g", c)][:, n0 : n0 + P, :].rearrange("p n (u e) -> p n u e", u=2)
+                src = view[:, b, :, :].rearrange("p u (n e) -> p n u e", e=2)
+                if on_scalar:
                     nc.scalar.activation(out=dst, in_=src, func=ACT.Relu)
                 else:
                     nc.vector.tensor_scalar_max(out=dst, in0=src, scalar1=0.0)
 
-        def h0_quant(c, lo=0, hi=CH):
+        def h0_quant(c, lo, n):
             nc.vector.quantize_mx(
-                out=h0w[:, c, lo:hi].bitcast(FP8X4),
-                scales=h0s[:, c, lo:hi],
-                in_=st[("h0g", c)][:, lo:hi, :].rearrange("p n t -> p (n t)"),
+                out=h0w[:, c, lo : lo + n].bitcast(FP8X4),
+                scales=h0s[:, c, lo : lo + n],
+                in_=live[("h0g", c)][:, lo : lo + n, :].rearrange("p n t -> p (n t)"),
             )
 
-        def w1_regroup(s, lo=0, hi=H):
-            if lo == 0:
-                st[("w1g", s)] = work.tile([P, H, 4], BF16, align_bytes=64, tag="w1g", name="w1g")
+        def side_by_side(dst, src):
             nc.vector.tensor_copy(
-                out=st[("w1g", s)][:, lo:hi, :].rearrange("p (c i) t -> p c t i", i=4),
-                in_=w1raw[:, s, :, lo:hi].rearrange("p t (c i) -> p c t i", i=4),
+                out=dst.rearrange("p (c i) t -> p c t i", i=4), in_=src.rearrange("p t (c i) -> p c t i", i=4)
             )
 
-        def w1_quant(s, lo=0, hi=H):
+        def w1_regroup(s, lo, n):
+            if lo == 0:
+                live[("w1g", s)] = work.tile([P, H, PACK], BF16, align_bytes=64, tag="w1g", name="w1g")
+            side_by_side(live[("w1g", s)][:, lo : lo + n, :], w1raw[:, s, :, lo : lo + n])
+
+        def w1_quant(s, lo, n):
             nc.vector.quantize_mx(
-                out=w1w[:, s, lo:hi].bitcast(FP8X4),
-                scales=w1s[:, s, lo:hi],
-                in_=st[("w1g", s)][:, lo:hi, :].rearrange("p n t -> p (n t)"),
+                out=w1w[:, s, lo : lo + n].bitcast(FP8X4),
+                scales=w1s[:, s, lo : lo + n],
+                in_=live[("w1g", s)][:, lo : lo + n, :].rearrange("p n t -> p (n t)"),
             )
 
         def w2_regroup():
@@ -138,149 +154,188 @@ def tile_moe_pb_kernel(tc, encodings, alphas, W1, b1, W2, b2, out):
                 in_=w2g[:].rearrange("p s c t -> p (s c t)"),
             )
 
-        def mx1(k, t):
-            c, s = divmod(k, S)
-            ps1 = ps1p.tile([P, CH], F32, tag="ps1", name="ps1")
-            st[("ps1", k, t)] = ps1
+        def stage1(i, t):
+            c, s, lo, n = units[i]
+            acc1 = bank1.tile([P, CHUNK], F32, tag="acc1", name="acc1")
+            live[("acc1", i, t)] = acc1
             nc.tensor.matmul_mx(
-                out=ps1[:],
+                out=acc1[:, 0:n],
                 lhsT=w1w[:, s, P * t : P * t + P].bitcast(FP8X4),
                 lhsT_scale=w1s[:, s, P * t : P * t + P],
-                rhs=h0w[:, c, :].bitcast(FP8X4),
-                rhs_scale=h0s[:, c, :],
+                rhs=h0w[:, c, lo : lo + n].bitcast(FP8X4),
+                rhs_scale=h0s[:, c, lo : lo + n],
                 start=True,
                 stop=True,
             )
 
-        def ev(k, t):
-            s = k % S
+        def hidden(i, t):
+            s, n = units[i][1], units[i][3]
             if t == 0:
-                st[("planar", k)] = work.tile([P, 4, CH], BF16, tag="planar", name="planar", bufs=4)
+                live[("planes", i)] = work.tile([P, PACK, CHUNK], BF16, tag="planes", name="planes", bufs=4)
             nc.scalar.activation(
-                out=st[("planar", k)][:, t, :], in_=st[("ps1", k, t)][:], func=ACT.Relu,
-                bias=biasT[:, 4 * s + t : 4 * s + t + 1], scale=1.0,
+                out=live[("planes", i)][:, t, 0:n],
+                in_=live[("acc1", i, t)][:, 0:n],
+                func=ACT.Relu,
+                bias=biasT[:, PACK * s + t : PACK * s + t + 1],
+                scale=1.0,
             )
 
-        def rg(k):
-            h1g = work.tile([P, CH, 4], BF16, align_bytes=64, tag="h1g", name="h1g", bufs=2)
-            st[("h1g", k)] = h1g
-            nc.vector.tensor_copy(
-                out=h1g[:].rearrange("p (c i) t -> p c t i", i=4),
-                in_=st[("planar", k)][:].rearrange("p t (c i) -> p c t i", i=4),
-            )
+        def regroup(i):
+            n = units[i][3]
+            h1g = work.tile([P, CHUNK, PACK], BF16, align_bytes=64, tag="h1g", name="h1g", bufs=3)
+            live[("h1g", i)] = h1g
+            side_by_side(h1g[:, 0:n, :], live[("planes", i)][:, :, 0:n])
 
-        def qu(k):
-            h1w = work.tile([P, CH], U32, align_bytes=64, tag="h1w", name="h1w", bufs=3)
-            h1s = work.tile([P, CH], U8, align_bytes=64, tag="h1s", name="h1s", bufs=3)
-            st[("h1w", k)] = h1w
-            st[("h1s", k)] = h1s
+        def quantise(i):
+            n = units[i][3]
+            h1w = work.tile([P, CHUNK], U32, align_bytes=64, tag="h1w", name="h1w", bufs=4)
+            h1s = work.tile([P, CHUNK], U8, align_bytes=64, tag="h1s", name="h1s", bufs=4)
+            live[("h1w", i)] = h1w
+            live[("h1s", i)] = h1s
             nc.vector.quantize_mx(
-                out=h1w[:].bitcast(FP8X4), scales=h1s[:], in_=st[("h1g", k)][:].rearrange("p n t -> p (n t)")
+                out=h1w[:, 0:n].bitcast(FP8X4),
+                scales=h1s[:, 0:n],
+                in_=live[("h1g", i)][:, 0:n, :].rearrange("p n t -> p (n t)"),
             )
 
-        def mx2(k):
-            s = k % S
-            ps2 = ps2p.tile([P, CH], F32, tag="ps2", name="ps2")
-            st[("ps2", k)] = ps2
+        def stage2(i, pool, tag):
+            s, n = units[i][1], units[i][3]
+            acc2 = pool.tile([P, CHUNK], F32, tag=tag, name="acc2")
+            live[("acc2", i)] = acc2
             nc.tensor.matmul_mx(
-                out=ps2[:],
+                out=acc2[:, 0:n],
                 lhsT=w2w[:, s, :].bitcast(FP8X4),
                 lhsT_scale=w2s[:, s, :],
-                rhs=st[("h1w", k)][:].bitcast(FP8X4),
-                rhs_scale=st[("h1s", k)][:],
+                rhs=live[("h1w", i)][:, 0:n].bitcast(FP8X4),
+                rhs_scale=live[("h1s", i)][:, 0:n],
                 start=True,
                 stop=True,
             )
 
-        def sg(k):
-            s = k % S
-            prob = work.tile([P, CH], F32, tag="prob", name="prob", bufs=2)
-            st[("prob", k)] = prob
+        def sigmoid(i):
+            s, n = units[i][1], units[i][3]
+            prob = work.tile([P, CHUNK], F32, tag="prob", name="prob", bufs=4)
+            live[("prob", i)] = prob
             nc.scalar.activation(
-                out=prob[:], in_=st[("ps2", k)][:], func=ACT.Sigmoid, bias=biasT[:, 16 + s : 17 + s], scale=1.0
+                out=prob[:, 0:n], in_=live[("acc2", i)][:, 0:n], func=ACT.Sigmoid,
+                bias=biasT[:, 16 + s : 17 + s], scale=1.0,
             )
 
-        def tr(k):
-            tq = tqp.tile([P, NB, T], F32, tag="tq", name="tq")
-            st[("tq", k)] = tq
-            for b in range(NB):
-                nc.tensor.transpose(tq[:, b, :], st[("prob", k)][:, P * b : P * b + P], ident_f[:])
+        def turn_back(i, pool, tag):
+            n = units[i][3]
+            back = pool.tile([P, BLOCKS, T], F32, tag=tag, name="back")
+            live[("back", i)] = back
+            for b in range(n // P):
+                nc.tensor.transpose(back[:, b, :], live[("prob", i)][:, P * b : P * b + P], ident_f[:])
 
-        def mix(k):
-            c, s = divmod(k, S)
+        def mix(i):
+            c, s, lo, n = units[i]
             if s == 0:
-                st[("acc", c)] = work.tile([P, NB, T], F32, tag="acc", name="acc")
-            acc = st[("acc", c)]
-            tq = st[("tq", k)]
-            for b in range(NB):
-                col = 32 * s + NB * c + b
-                if s == 0 and c % 2 == 0:
-                    nc.scalar.activation(out=acc[:, b, :], in_=tq[:, b, :], func=ACT.Copy, scale=alT[:, col : col + 1])
-                elif s == 0:
-                    nc.vector.tensor_scalar_mul(out=acc[:, b, :], in0=tq[:, b, :], scalar1=alT[:, col : col + 1])
+                live[("mixed", c)] = work.tile([P, BLOCKS, T], F32, tag="mixed", name="mixed")
+            mixed = live[("mixed", c)]
+            b0 = lo // P
+            for b in range(n // P):
+                col = (N_TOK // P) * s + BLOCKS * c + b0 + b
+                if s == 0:
+                    nc.vector.tensor_scalar_mul(
+                        out=mixed[:, b0 + b, :], in0=live[("back", i)][:, b, :], scalar1=alT[:, col : col + 1]
+                    )
                 else:
                     nc.vector.scalar_tensor_tensor(
-                        out=acc[:, b, :], in0=tq[:, b, :], scalar=alT[:, col : col + 1], in1=acc[:, b, :],
-                        op0=ALU.mult, op1=ALU.add,
+                        out=mixed[:, b0 + b, :],
+                        in0=live[("back", i)][:, b, :],
+                        scalar=alT[:, col : col + 1],
+                        in1=mixed[:, b0 + b, :],
+                        op0=ALU.mult,
+                        op1=ALU.add,
                     )
             if s == S - 1:
-                nc.sync.dma_start(out=out_v[c], in_=acc[:])
+                nc.sync.dma_start(out=out_v[c][:, b0 : b0 + n // P, :], in_=mixed[:, b0 : b0 + n // P, :])
 
         h0_transposes(0)
-        tb = ps2p.tile([P, P], BF16, tag="ps2", name="tb")
-        nc.tensor.transpose(tb[:], small[:], ident_b[:])
-        ta = tqp.tile([P, P], BF16, tag="tq", name="ta")
-        nc.tensor.transpose(ta[:], alraw[:], ident_b[:])
-        h0_evac(0, 0, "V")
-        h0_evac(0, 1, "S")
-        nc.vector.tensor_copy(out=biasT[:], in_=tb[:, 0:20])
-        h0_quant(0, 0, 256)
-        w1_regroup(0, 0, 128)
-        h0_quant(0, 256, 512)
-        w1_quant(0, 0, 128)
-        w1_regroup(0, 128, 256)
-        w1_regroup(0, 256, 384)
-        w1_quant(0, 128, 256)
-        w1_regroup(0, 384, 512)
-        w1_quant(0, 256, 384)
-        nc.vector.tensor_copy(out=alT[:], in_=ta[:])
-        w1_quant(0, 384, 512)
-        for t in range(4):
-            mx1(0, t)
+        smallT = bank2.tile([P, P], BF16, tag="acc2", name="smallT")
+        nc.tensor.transpose(smallT[:], small[:], ident_b[:])
+        alphaT = bankp.tile([P, P], BF16, tag="back", name="alphaT")
+        nc.tensor.transpose(alphaT[:], alraw[:], ident_b[:])
+        h0_copy(0, 0, False)
+        h0_copy(0, 1, True)
+        nc.vector.tensor_copy(out=biasT[:], in_=smallT[:, 0:20])
+        h0_quant(0, 0, HALF)
+        w1_regroup(0, 0, P)
+        h0_quant(0, HALF, HALF)
+        w1_quant(0, 0, P)
+        w1_regroup(0, P, P)
+        w1_regroup(0, 2 * P, P)
+        w1_quant(0, P, P)
+        w1_regroup(0, 3 * P, P)
+        w1_quant(0, 2 * P, P)
+        nc.vector.tensor_copy(out=alT[:], in_=alphaT[:])
+        w1_quant(0, 3 * P, P)
+        for t in range(PACK):
+            stage1(0, t)
 
-        for k in range(NU + 3):
-            c, s = divmod(k, S)
-            nxt = c + 1 if (k < NU and c + 1 < NCH) else None
-            if 0 <= k - 3 < NU:
-                tr(k - 3)
-            if nxt is not None and s == (2 if c == 0 else 1):
-                h0_transposes(nxt)
-            if 0 <= k - 2 < NU:
-                mx2(k - 2)
+        for k in range(n_whole):
+            c, s = units[k][0], units[k][1]
+            turn_at = 2 if c == 0 else 1
+            prepare = c + 1 < N_CHUNKS
+            if k >= 3:
+                turn_back(k - 3, bankp, "back")
+            if prepare and s == turn_at:
+                h0_transposes(c + 1)
+            if k >= 2:
+                stage2(k - 2, bank2, "acc2")
             if k + 1 < S:
-                w1_regroup(k + 1)
-            if 0 <= k - 1 < NU:
-                rg(k - 1)
+                w1_regroup(k + 1, 0, H)
+            if k >= 1:
+                regroup(k - 1)
             if k == 1:
                 w2_regroup()
-            if nxt is not None and s == (3 if c == 0 else 2):
-                h0_quant(nxt)
+            if prepare and s == turn_at + 1:
+                h0_quant(c + 1, 0, CHUNK)
             if k + 1 < S:
-                w1_quant(k + 1)
-            for t in range(4):
-                if k < NU:
-                    ev(k, t)
-                if k + 1 < NU:
-                    mx1(k + 1, t)
-            if 0 <= k - 3 < NU:
+                w1_quant(k + 1, 0, H)
+            for t in range(PACK):
+                hidden(k, t)
+                stage1(k + 1, t)
+            if k >= 3:
                 mix(k - 3)
-            if nxt is not None and s == (2 if c == 0 else 1):
-                engs = ("V", "V")
-                h0_evac(nxt, 0, engs[0])
-                h0_evac(nxt, 1, engs[1])
-            if 0 <= k - 1 < NU:
-                qu(k - 1)
+            if prepare and s == turn_at:
+                h0_copy(c + 1, 0, False)
+                h0_copy(c + 1, 1, False)
+            if k >= 1:
+                quantise(k - 1)
             if k == 1:
                 w2_quant()
-            if 0 <= k - 2 < NU:
-                sg(k - 2)
+            if k >= 2:
+                sigmoid(k - 2)
+
+        a, b = n_whole, n_whole + 1
+        turn_back(a - 3, bankp, "back")
+        stage2(a - 2, bank2, "acc2")
+        regroup(a - 1)
+        for t in range(PACK):
+            hidden(a, t)
+            stage1(b, t)
+        for t in range(PACK):
+            hidden(b, t)
+        mix(a - 3)
+        quantise(a - 1)
+        sigmoid(a - 2)
+        stage2(a - 1, bank1, "acc1")
+        regroup(a)
+        regroup(b)
+        turn_back(a - 2, bankp, "back")
+        sigmoid(a - 1)
+        quantise(a)
+        stage2(a, bank1, "acc1")
+        quantise(b)
+        stage2(b, bank1, "acc1")
+        mix(a - 2)
+        turn_back(a - 1, bank1, "acc1")
+        sigmoid(a)
+        sigmoid(b)
+        mix(a - 1)
+        turn_back(a, bank2, "acc2")
+        mix(a)
+        turn_back(b, bankp, "back")
+        mix(b)

from contextlib import ExitStack

import concourse.mybir as mybir
from concourse.masks import make_identity

F32 = mybir.dt.float32
BF16 = mybir.dt.bfloat16
U32 = mybir.dt.uint32
U8 = mybir.dt.uint8
FP8X4 = mybir.dt.float8_e4m3fn_x4
ACT = mybir.ActivationFunctionType
ALU = mybir.AluOpType

P = 128
PACK = 4
N_TOK, H, S, T = 4096, 512, 4, 128
CHUNK = 512
BLOCKS = CHUNK // P
N_CHUNKS = N_TOK // CHUNK
HALF = CHUNK // 2
FLOPS = 2 * S * N_TOK * H * (H + T)


def tile_moe_pb_kernel(tc, encodings, alphas, W1, b1, W2, b2, out):
    nc = tc.nc
    with ExitStack() as ctx:
        ctx.enter_context(tc.manual_schedule())
        const = ctx.enter_context(tc.tile_pool(name="const", bufs=1))
        work = ctx.enter_context(tc.tile_pool(name="work", bufs=2))
        bank1 = ctx.enter_context(tc.psum_pool(name="bank1", bufs=PACK))
        bank2 = ctx.enter_context(tc.psum_pool(name="bank2", bufs=1))
        bankp = ctx.enter_context(tc.psum_pool(name="bankp", bufs=1))
        bankx = ctx.enter_context(tc.psum_pool(name="bankx", bufs=2))

        units = []
        for c in range(N_CHUNKS):
            for s in range(S):
                if c == N_CHUNKS - 1 and s == S - 1:
                    units.append((c, s, 0, HALF))
                    units.append((c, s, HALF, HALF))
                else:
                    units.append((c, s, 0, CHUNK))
        n_whole = len(units) - 2

        enc_v = encodings.rearrange("(c b p) k -> c p b k", p=P, b=BLOCKS)
        out_v = out.rearrange("(c b p) t -> c p b t", p=P, b=BLOCKS)
        w1raw = const.tile([P, S, PACK, H], BF16)
        w2raw = const.tile([P, S, PACK, T], BF16)
        small = const.tile([P, P], BF16)
        alraw = const.tile([P, P], BF16)
        zero = const.tile([P, 1], F32)
        warm = const.tile([P, 1], F32)
        nc.vector.memset(small[:], 0.0)
        nc.vector.memset(zero[:], 0.0)
        xs = []
        for c in range(N_CHUNKS):
            x_c = const.tile([P, BLOCKS, H], BF16, name="x%d" % c)
            xs.append(x_c)

        def load_w1(s):
            nc.sync.dma_start(
                out=w1raw[:, s, :, :].rearrange("p (u e) j -> p u (e j)", u=2),
                in_=W1[s].rearrange("(u q e) j -> q u (e j)", u=2, e=2),
            )

        nc.scalar.dma_start(out=small[0:16, :], in_=b1.rearrange("s (t p) -> (s t) p", p=P))
        nc.scalar.dma_start(out=small[16:20, :], in_=b2)
        nc.scalar.dma_start(out=alraw[:], in_=alphas.rearrange("s (n p) -> (s n) p", p=P))
        nc.sync.dma_start(out=xs[0][:, 0:2, :], in_=enc_v[0][:, 0:2, :])
        nc.sync.dma_start(out=xs[0][:, 2:4, :], in_=enc_v[0][:, 2:4, :])
        load_w1(0)
        load_w1(1)
        nc.sync.dma_start(
            out=w2raw[:].rearrange("p s t c -> p (s t) c"), in_=W2.rearrange("s (t p) c -> p (s t) c", p=P)
        )
        load_w1(2)
        nc.sync.dma_start(out=xs[1][:], in_=enc_v[1])
        load_w1(3)
        for c in range(2, N_CHUNKS):
            nc.sync.dma_start(out=xs[c][:], in_=enc_v[c])

        ident_f = const.tile([P, P], F32)
        make_identity(nc, ident_f[:])
        ident_b = const.tile([P, P], BF16)
        make_identity(nc, ident_b[:])
        nc.scalar.activation(out=warm[:], in_=zero[:], func=ACT.Sigmoid)

        w1w = const.tile([P, S, H], U32, align_bytes=64)
        w1s = const.tile([P, S, H], U8, align_bytes=64)
        w2w = const.tile([P, S, T], U32, align_bytes=64)
        w2s = const.tile([P, S, T], U8, align_bytes=64)
        w2g = const.tile([P, S, T, PACK], BF16, align_bytes=64)
        h0w = const.tile([P, N_CHUNKS, CHUNK], U32, align_bytes=64)
        h0s = const.tile([P, N_CHUNKS, CHUNK], U8, align_bytes=64)
        biasT = const.tile([P, 20], F32)
        alT = const.tile([P, P], F32)

        live = {}

        def h0_transposes(c):
            words = xs[c][:].bitcast(F32)
            for pair in range(2):
                turned = bankx.tile([P, 2, 2, P], F32, tag="turned", name="turned")
                live[("turned", c, pair)] = turned
                for b in range(2):
                    for u in range(2):
                        nc.tensor.transpose(
                            turned[:, b, u, :], words[:, 2 * pair + b, P * u : P * u + P], ident_f[:]
                        )
            live[("h0g", c)] = work.tile([P, CHUNK, PACK], BF16, align_bytes=64, tag="h0g", name="h0g")

        def h0_copy(c, pair, on_scalar):
            view = live[("turned", c, pair)][:].bitcast(BF16)
            for b in range(2):
                n0 = P * (2 * pair + b)
                dst = live[("h0g", c)][:, n0 : n0 + P, :].rearrange("p n (u e) -> p n u e", u=2)
                src = view[:, b, :, :].rearrange("p u (n e) -> p n u e", e=2)
                if on_scalar:
                    nc.scalar.activation(out=dst, in_=src, func=ACT.Relu)
                else:
                    nc.vector.tensor_scalar_max(out=dst, in0=src, scalar1=0.0)

        def h0_quant(c, lo, n):
            nc.vector.quantize_mx(
                out=h0w[:, c, lo : lo + n].bitcast(FP8X4),
                scales=h0s[:, c, lo : lo + n],
                in_=live[("h0g", c)][:, lo : lo + n, :].rearrange("p n t -> p (n t)"),
            )

        def side_by_side(dst, src):
            nc.vector.tensor_copy(
                out=dst.rearrange("p (c i) t -> p c t i", i=4), in_=src.rearrange("p t (c i) -> p c t i", i=4)
            )

        def w1_regroup(s, lo, n):
            if lo == 0:
                live[("w1g", s)] = work.tile([P, H, PACK], BF16, align_bytes=64, tag="w1g", name="w1g")
            side_by_side(live[("w1g", s)][:, lo : lo + n, :], w1raw[:, s, :, lo : lo + n])

        def w1_quant(s, lo, n):
            nc.vector.quantize_mx(
                out=w1w[:, s, lo : lo + n].bitcast(FP8X4),
                scales=w1s[:, s, lo : lo + n],
                in_=live[("w1g", s)][:, lo : lo + n, :].rearrange("p n t -> p (n t)"),
            )

        def w2_regroup():
            nc.scalar.copy(out=w2g[:], in_=w2raw[:].rearrange("p s t c -> p s c t"))

        def w2_quant():
            nc.vector.quantize_mx(
                out=w2w[:].rearrange("p s c -> p (s c)").bitcast(FP8X4),
                scales=w2s[:].rearrange("p s c -> p (s c)"),
                in_=w2g[:].rearrange("p s c t -> p (s c t)"),
            )

        def stage1(i, t):
            c, s, lo, n = units[i]
            acc1 = bank1.tile([P, CHUNK], F32, tag="acc1", name="acc1")
            live[("acc1", i, t)] = acc1
            nc.tensor.matmul_mx(
                out=acc1[:, 0:n],
                lhsT=w1w[:, s, P * t : P * t + P].bitcast(FP8X4),
                lhsT_scale=w1s[:, s, P * t : P * t + P],
                rhs=h0w[:, c, lo : lo + n].bitcast(FP8X4),
                rhs_scale=h0s[:, c, lo : lo + n],
                start=True,
                stop=True,
            )

        def hidden(i, t):
            s, n = units[i][1], units[i][3]
            if t == 0:
                live[("planes", i)] = work.tile([P, PACK, CHUNK], BF16, tag="planes", name="planes", bufs=4)
            nc.scalar.activation(
                out=live[("planes", i)][:, t, 0:n],
                in_=live[("acc1", i, t)][:, 0:n],
                func=ACT.Relu,
                bias=biasT[:, PACK * s + t : PACK * s + t + 1],
                scale=1.0,
            )

        def regroup(i):
            n = units[i][3]
            h1g = work.tile([P, CHUNK, PACK], BF16, align_bytes=64, tag="h1g", name="h1g", bufs=3)
            live[("h1g", i)] = h1g
            side_by_side(h1g[:, 0:n, :], live[("planes", i)][:, :, 0:n])

        def quantise(i):
            n = units[i][3]
            h1w = work.tile([P, CHUNK], U32, align_bytes=64, tag="h1w", name="h1w", bufs=4)
            h1s = work.tile([P, CHUNK], U8, align_bytes=64, tag="h1s", name="h1s", bufs=4)
            live[("h1w", i)] = h1w
            live[("h1s", i)] = h1s
            nc.vector.quantize_mx(
                out=h1w[:, 0:n].bitcast(FP8X4),
                scales=h1s[:, 0:n],
                in_=live[("h1g", i)][:, 0:n, :].rearrange("p n t -> p (n t)"),
            )

        def stage2(i, pool, tag):
            s, n = units[i][1], units[i][3]
            acc2 = pool.tile([P, CHUNK], F32, tag=tag, name="acc2")
            live[("acc2", i)] = acc2
            nc.tensor.matmul_mx(
                out=acc2[:, 0:n],
                lhsT=w2w[:, s, :].bitcast(FP8X4),
                lhsT_scale=w2s[:, s, :],
                rhs=live[("h1w", i)][:, 0:n].bitcast(FP8X4),
                rhs_scale=live[("h1s", i)][:, 0:n],
                start=True,
                stop=True,
            )

        def sigmoid(i):
            s, n = units[i][1], units[i][3]
            prob = work.tile([P, CHUNK], F32, tag="prob", name="prob", bufs=4)
            live[("prob", i)] = prob
            nc.scalar.activation(
                out=prob[:, 0:n], in_=live[("acc2", i)][:, 0:n], func=ACT.Sigmoid,
                bias=biasT[:, 16 + s : 17 + s], scale=1.0,
            )

        def turn_back(i, pool, tag):
            n = units[i][3]
            back = pool.tile([P, BLOCKS, T], F32, tag=tag, name="back")
            live[("back", i)] = back
            for b in range(n // P):
                nc.tensor.transpose(back[:, b, :], live[("prob", i)][:, P * b : P * b + P], ident_f[:])

        def mix(i):
            c, s, lo, n = units[i]
            if s == 0:
                live[("mixed", c)] = work.tile([P, BLOCKS, T], F32, tag="mixed", name="mixed")
            mixed = live[("mixed", c)]
            b0 = lo // P
            for b in range(n // P):
                col = (N_TOK // P) * s + BLOCKS * c + b0 + b
                if s == 0:
                    nc.vector.tensor_scalar_mul(
                        out=mixed[:, b0 + b, :], in0=live[("back", i)][:, b, :], scalar1=alT[:, col : col + 1]
                    )
                else:
                    nc.vector.scalar_tensor_tensor(
                        out=mixed[:, b0 + b, :],
                        in0=live[("back", i)][:, b, :],
                        scalar=alT[:, col : col + 1],
                        in1=mixed[:, b0 + b, :],
                        op0=ALU.mult,
                        op1=ALU.add,
                    )
            if s == S - 1:
                nc.sync.dma_start(out=out_v[c][:, b0 : b0 + n // P, :], in_=mixed[:, b0 : b0 + n // P, :])

        h0_transposes(0)
        smallT = bank2.tile([P, P], BF16, tag="acc2", name="smallT")
        nc.tensor.transpose(smallT[:], small[:], ident_b[:])
        alphaT = bankp.tile([P, P], BF16, tag="back", name="alphaT")
        nc.tensor.transpose(alphaT[:], alraw[:], ident_b[:])
        h0_copy(0, 0, False)
        h0_copy(0, 1, True)
        nc.vector.tensor_copy(out=biasT[:], in_=smallT[:, 0:20])
        h0_quant(0, 0, HALF)
        w1_regroup(0, 0, P)
        h0_quant(0, HALF, HALF)
        w1_quant(0, 0, P)
        w1_regroup(0, P, P)
        w1_regroup(0, 2 * P, P)
        w1_quant(0, P, P)
        w1_regroup(0, 3 * P, P)
        w1_quant(0, 2 * P, P)
        nc.vector.tensor_copy(out=alT[:], in_=alphaT[:])
        w1_quant(0, 3 * P, P)
        for t in range(PACK):
            stage1(0, t)

        for k in range(n_whole):
            c, s = units[k][0], units[k][1]
            turn_at = 2 if c == 0 else 1
            prepare = c + 1 < N_CHUNKS
            if k >= 3:
                turn_back(k - 3, bankp, "back")
            if prepare and s == turn_at:
                h0_transposes(c + 1)
            if k >= 2:
                stage2(k - 2, bank2, "acc2")
            if k + 1 < S:
                w1_regroup(k + 1, 0, H)
            if k >= 1:
                regroup(k - 1)
            if k == 1:
                w2_regroup()
            if prepare and s == turn_at + 1:
                h0_quant(c + 1, 0, CHUNK)
            if k + 1 < S:
                w1_quant(k + 1, 0, H)
            for t in range(PACK):
                hidden(k, t)
                stage1(k + 1, t)
            if k >= 3:
                mix(k - 3)
            if prepare and s == turn_at:
                h0_copy(c + 1, 0, False)
                h0_copy(c + 1, 1, False)
            if k >= 1:
                quantise(k - 1)
            if k == 1:
                w2_quant()
            if k >= 2:
                sigmoid(k - 2)

        a, b = n_whole, n_whole + 1
        turn_back(a - 3, bankp, "back")
        stage2(a - 2, bank2, "acc2")
        regroup(a - 1)
        for t in range(PACK):
            hidden(a, t)
            stage1(b, t)
        for t in range(PACK):
            hidden(b, t)
        mix(a - 3)
        quantise(a - 1)
        sigmoid(a - 2)
        stage2(a - 1, bank1, "acc1")
        regroup(a)
        regroup(b)
        turn_back(a - 2, bankp, "back")
        sigmoid(a - 1)
        quantise(a)
        stage2(a, bank1, "acc1")
        quantise(b)
        stage2(b, bank1, "acc1")
        mix(a - 2)
        turn_back(a - 1, bank1, "acc1")
        sigmoid(a)
        sigmoid(b)
        mix(a - 1)
        turn_back(a, bank2, "acc2")
        mix(a)
        turn_back(b, bankp, "back")
        mix(b)
